import numpy as np
import ml_dtypes


def mxq(x, axis, fmt="e4m3"):
    dtype, down = {"e4m3": (ml_dtypes.float8_e4m3fn, 7), "e5m2": (ml_dtypes.float8_e5m2, 14)}[fmt]
    v = np.moveaxis(np.asarray(x, np.float32).astype(ml_dtypes.bfloat16).astype(np.float64), axis, -1)
    blocks = v.reshape(v.shape[:-1] + (-1, 32))
    amax = np.abs(blocks).max(-1, keepdims=True)
    byte = np.maximum(np.where(amax > 0, np.frexp(amax)[1] - 1 + 127, 0) - down, 1)
    scale = np.exp2(byte - 127.0)
    codes = (blocks / scale).astype(np.float32).astype(dtype).astype(np.float64)
    return np.moveaxis((codes * scale).reshape(v.shape), -1, axis)


WIDE = False


def mx_kscale(k):
    if not WIDE:
        return np.ones(k)
    levels = np.array([10, -10, 5, -5, 0])
    a = np.random.permutation(np.resize(levels, k // 512 * 4)).reshape(k // 512, 4)
    idx = np.arange(k)
    return np.exp2(a[idx // 512, idx % 128 // 32])


BF16 = ml_dtypes.bfloat16


def bf(x):
    return np.asarray(x, np.float32).astype(BF16)


def f64(x):
    return np.asarray(x).astype(np.float64)


E, H, D = 2, 1024, 2048
B, S = 2, 128
ALPHA = 1.702
LIMIT = 7.0


def sigmoid(v):
    return 1.0 / (1.0 + np.exp(-v))


def setup_inputs():
    s = mx_kscale(H)
    return {
        "hidden_states": bf(np.random.standard_normal((B, S, H)) * s),
        "routing_weights": bf(np.random.random_sample((B * S, E))),
        "gate_up_proj": bf(np.random.standard_normal((E, H, 2 * D)) * 0.08 / s[None, :, None]),
        "gate_up_proj_bias": bf(np.random.standard_normal((E, 2 * D)) * 0.5),
        "down_proj": bf(np.random.standard_normal((E, D, H)) * 0.006),
        "down_proj_bias": bf(np.random.standard_normal((E, H)) * 0.5),
    }


def reference(hidden_states, routing_weights, gate_up_proj, gate_up_proj_bias, down_proj, down_proj_bias):
    b, s, h = hidden_states.shape
    x = f64(hidden_states).reshape(-1, h)
    xq = mxq(x, 1, "e4m3")
    gate_up = (xq[None, :, :] @ mxq(f64(gate_up_proj), 1, "e4m3")) + f64(gate_up_proj_bias)[:, None, :]
    gate = gate_up[..., ::2]
    up = gate_up[..., 1::2]
    gate = np.minimum(gate, LIMIT)
    up = np.clip(up, -LIMIT, LIMIT)
    glu = gate * sigmoid(gate * ALPHA)
    hid = (up + 1.0) * glu
    nxt = mxq(hid, 2, "e4m3") @ mxq(f64(down_proj), 1, "e4m3")
    nxt = nxt + f64(down_proj_bias)[:, None, :]
    nxt = nxt * f64(routing_weights).T[:, :, None]
    out = nxt.sum(axis=0).reshape(b, s, h)
    return out

@@ -1,0 +1,388 @@
+import math
+from contextlib import ExitStack
+
+import concourse.mybir as mybir
+from concourse.masks import make_identity
+
+FLOPS = 2 * 2 * 256 * 1024 * 4096 + 2 * 2 * 256 * 2048 * 1024
+
+BF16 = mybir.dt.bfloat16
+F32 = mybir.dt.float32
+I32 = mybir.dt.int32
+U32 = mybir.dt.uint32
+U8 = mybir.dt.uint8
+FP8X4 = mybir.dt.float8_e4m3fn_x4
+ACT = mybir.ActivationFunctionType
+ALU = mybir.AluOpType
+
+P = 128
+ALPHA = 1.702
+LIMIT = 7.0
+GLU_CAP = LIMIT / (1.0 + math.exp(-ALPHA * LIMIT))
+
+PIN = True
+RAW_BUFS = 5
+NV_A = 512
+NV_D = 512
+LAG_ACT = 2
+LAG_EPI = 4
+HEAD_SLOTS = 4
+
+
+def tile_referenceexperts_kernel(
+    tc,
+    hidden_states,
+    routing_weights,
+    gate_up_proj,
+    gate_up_proj_bias,
+    down_proj,
+    down_proj_bias,
+    out,
+):
+    nc = tc.nc
+    with ExitStack() as ctx:
+        const = ctx.enter_context(tc.tile_pool(name="const", bufs=1))
+        rawp = ctx.enter_context(tc.tile_pool(name="rawp", bufs=RAW_BUFS))
+        grpp = ctx.enter_context(tc.tile_pool(name="grpp", bufs=4))
+        codep = ctx.enter_context(tc.tile_pool(name="codep", bufs=8))
+        epip = ctx.enter_context(tc.tile_pool(name="epip", bufs=2))
+        hidp = ctx.enter_context(tc.tile_pool(name="hidp", bufs=8))
+        ps1p = ctx.enter_context(tc.psum_pool(name="ps1p", bufs=4))
+        accp = ctx.enter_context(tc.psum_pool(name="accp", bufs=1))
+        if PIN:
+            ctx.enter_context(tc.manual_schedule())
+
+        wgu = gate_up_proj.rearrange("e (r p) n -> e p r n", p=P)
+        wd = down_proj.rearrange("e (r p) h -> e p r h", p=P)
+        out_v = out.rearrange("b s h -> s b h")
+
+        units = []
+        for e in range(2):
+            for g in range(4):
+                for c in range(2):
+                    units.append(("A", e, g, c))
+            for g in range(4):
+                units.append(("D", e, g, 0))
+        n_units = len(units)
+        n_chunks = n_units // 2
+
+        raw_of = {}
+        grp_of = {}
+        codes_of = {}
+        ps_of = {}
+        gr_of = {}
+        hg_of = {}
+        hid_of = {}
+        acc_of = {}
+
+        r_stage = const.tile([P, 2, 2], BF16, name="r_stage")
+        bias_stage = const.tile([32, 256], BF16, name="bias_stage")
+        bd_stage = const.tile([2, 1024], BF16, name="bd_stage")
+        nc.scalar.dma_start(
+            out=r_stage[:], in_=routing_weights.rearrange("(i p) e -> p i e", p=P)
+        )
+        nc.scalar.dma_start(
+            out=bias_stage[:],
+            in_=gate_up_proj_bias.rearrange("e (r q) -> (e r) q", q=256),
+        )
+        nc.scalar.dma_start(out=bd_stage[:], in_=down_proj_bias)
+
+        zero1 = const.tile([P, 1], F32, name="zero1")
+        nc.vector.memset(zero1[:], 0.0)
+        warm = const.tile([P, 1], F32, name="warm")
+        nc.scalar.activation(out=warm[:], in_=zero1[:], func=ACT.Gelu_apprx_sigmoid)
+
+        bias_d = const.tile([P, 256], BF16, name="bias_d")
+        r_pad = const.tile([P, 256], BF16, name="r_pad")
+        bd_pad = const.tile([P, 1024], BF16, name="bd_pad")
+        nc.vector.memset(r_pad[:].bitcast(I32), 0)
+        nc.vector.memset(bias_d[:].bitcast(I32), 0)
+        nc.vector.memset(bd_pad[:].bitcast(I32), 0)
+        r_pad_v = r_pad.rearrange("p (i k) -> p i k", i=2)
+        bias_d_v = bias_d.rearrange("p (s m) -> p s m", s=2)
+
+        ident = const.tile([P, P], BF16, name="ident")
+        make_identity(nc, ident[:])
+
+        def chunk_src(k):
+            e, kk = divmod(k, n_chunks // 2)
+            if kk < 4:
+                return wgu[e, :, :, 1024 * kk : 1024 * kk + 1024]
+            return wd[e, :, 8 * (kk - 4) : 8 * (kk - 4) + 8, :]
+
+        def new_chunk(k):
+            raw_of[k] = rawp.tile([P, 8, 1024], BF16, name="raw")
+
+        def load_piece(k, r0, r1, c0, c1):
+            nc.sync.dma_start(
+                out=raw_of[k][:, r0:r1, c0:c1], in_=chunk_src(k)[:, r0:r1, c0:c1]
+            )
+
+        def load_chunk(k):
+            new_chunk(k)
+            load_piece(k, 0, 8, 0, 1024)
+
+        def regroup(u):
+            kind = units[u][0]
+            half = u % 2
+            src = raw_of[u // 2][:, 4 * half : 4 * half + 4, :]
+            grp = grpp.tile([P, 4096], BF16, name="grp", align_bytes=64)
+            grp_of[u] = grp
+            if kind == "A":
+                sv = src.rearrange("p t (q i s) -> p s q t i", i=4, s=2)
+                dv = grp.rearrange("p (s q i t) -> p s q t i", s=2, i=4, t=4)
+                qv = NV_A // 8
+                for s in range(2):
+                    nc.scalar.copy(out=dv[:, s, qv:], in_=sv[:, s, qv:])
+                for s in range(2):
+                    nc.vector.tensor_copy(out=dv[:, s, :qv], in_=sv[:, s, :qv])
+            else:
+                sv = src.rearrange("p t (q i) -> p q t i", i=4)
+                dv = grp.rearrange("p (q i t) -> p q t i", i=4, t=4)
+                qv = NV_D // 4
+                nc.scalar.copy(out=dv[:, qv:], in_=sv[:, qv:])
+                nc.vector.tensor_copy(out=dv[:, :qv], in_=sv[:, :qv])
+
+        def quantise(u, parts):
+            grp = grp_of[u]
+            cw = codep.tile([P, 1024], U32, name="cw", align_bytes=64)
+            cs = codep.tile([P, 1024], U8, name="cs", align_bytes=64)
+            codes_of[u] = (cw, cs)
+            w = 1024 // parts
+            for h in range(parts):
+                nc.vector.quantize_mx(
+                    out=cw[:, w * h : w * h + w].bitcast(FP8X4),
+                    scales=cs[:, w * h : w * h + w],
+                    in_=grp[:, 4 * w * h : 4 * w * h + 4 * w],
+                )
+
+        def stage1(e, g, u):
+            tiles = []
+            for j in range(4):
+                ps = ps1p.tile([P, 2, 256], F32, name="ps1", tag="ps1")
+                tiles.append(ps)
+                for s in range(2):
+                    off = 512 * s + P * j
+                    for c in range(2):
+                        cw, cs = codes_of[u - 1 + c]
+                        nc.tensor.matmul_mx(
+                            out=ps[:, s, :],
+                            lhsT=cw[:, off : off + P].bitcast(FP8X4),
+                            lhsT_scale=cs[:, off : off + P],
+                            rhs=xw[:, 256 * c : 256 * c + 256].bitcast(FP8X4),
+                            rhs_scale=xs[:, 256 * c : 256 * c + 256],
+                            start=(c == 0),
+                            stop=(c == 1),
+                        )
+            ps_of[(e, g)] = tiles
+
+        def acts(e, g):
+            gt = epip.tile([P, 4, 256], F32, name="gt")
+            rt = epip.tile([P, 4, 256], F32, name="rt")
+            gr_of[(e, g)] = (gt, rt)
+            for j in range(4):
+                ps = ps_of[(e, g)][j]
+                col = 16 * e + 4 * g + j
+                nc.scalar.activation(
+                    out=gt[:, j, :],
+                    in_=ps[:, 0, :],
+                    func=ACT.Gelu_apprx_sigmoid,
+                    bias=bg[:, col : col + 1],
+                )
+                nc.scalar.activation(
+                    out=rt[:, j, :],
+                    in_=ps[:, 1, :],
+                    func=ACT.Relu,
+                    bias=b7[:, col : col + 1],
+                )
+
+        def epilogue(e, g):
+            gt, rt = gr_of[(e, g)]
+            nc.vector.tensor_scalar(
+                out=rt[:],
+                in0=rt[:],
+                scalar1=2.0 * LIMIT,
+                scalar2=1.0 - LIMIT,
+                op0=ALU.min,
+                op1=ALU.add,
+            )
+            hf = epip.tile([P, 4, 256], BF16, name="hf")
+            nc.vector.scalar_tensor_tensor(
+                out=hf[:],
+                in0=gt[:],
+                scalar=GLU_CAP,
+                in1=rt[:],
+                op0=ALU.min,
+                op1=ALU.mult,
+            )
+            hg = epip.tile([P, 1024], BF16, name="hg", align_bytes=64)
+            hg_of[(e, g)] = hg
+            nc.vector.tensor_copy(
+                out=hg.rearrange("p (q i j) -> p q j i", i=4, j=4),
+                in_=hf.rearrange("p j (q i) -> p q j i", i=4),
+            )
+
+        def hid_quantise(e, g):
+            hw = hidp.tile([P, 256], U32, name="hw", align_bytes=64)
+            hs = hidp.tile([P, 256], U8, name="hs", align_bytes=64)
+            hid_of[(e, g)] = (hw, hs)
+            nc.vector.quantize_mx(
+                out=hw[:].bitcast(FP8X4), scales=hs[:], in_=hg_of[(e, g)][:]
+            )
+
+        def new_acc():
+            for k in range(4):
+                acc_of[k] = accp.tile([P, 512], F32, name="acc%d" % k)
+
+        def stage2(e, g, u):
+            if g == 0:
+                new_acc()
+            hw, hs = hid_of[(e, g)]
+            cw, cs = codes_of[u]
+            for k in range(4):
+                hh, i = divmod(k, 2)
+                nc.tensor.matmul_mx(
+                    out=acc_of[k][:],
+                    lhsT=hw[:, P * i : P * i + P].bitcast(FP8X4),
+                    lhsT_scale=hs[:, P * i : P * i + P],
+                    rhs=cw[:, 512 * hh : 512 * hh + 512].bitcast(FP8X4),
+                    rhs_scale=cs[:, 512 * hh : 512 * hh + 512],
+                    start=(g == 0),
+                    stop=(g == 3),
+                )
+
+        def finals(e):
+            for k in range(4):
+                hh, i = divmod(k, 2)
+                sl = slice(512 * hh, 512 * hh + 512)
+                nc.vector.scalar_tensor_tensor(
+                    out=b_sb[:, i, sl],
+                    in0=acc_of[k][:],
+                    scalar=rf[:, i, e : e + 1],
+                    in1=b_sb[:, i, sl],
+                    op0=ALU.mult,
+                    op1=ALU.add,
+                )
+                if e == 1:
+                    nc.sync.dma_start(out=out_v[:, i, sl], in_=b_sb[:, i, sl])
+
+        x_sb = const.tile([P, 2, 1024], BF16, name="x_sb")
+        new_chunk(0)
+        load_piece(0, 0, 4, NV_A, 1024)
+        load_piece(0, 0, 4, 0, NV_A)
+        nc.sync.dma_start(out=x_sb[:], in_=hidden_states.rearrange("b s h -> s b h"))
+        load_piece(0, 4, 8, 0, 1024)
+        new_chunk(1)
+        load_piece(1, 0, 4, 0, 1024)
+        load_piece(1, 4, 8, 0, 1024)
+        for k in range(2, RAW_BUFS):
+            load_chunk(k)
+
+        nc.vector.tensor_copy(out=r_pad_v[:, :, 0:2], in_=r_stage[:])
+        nc.vector.tensor_copy(
+            out=bias_d_v[0:32, :, :],
+            in_=bias_stage.rearrange("p (m s) -> p s m", s=2),
+        )
+        nc.vector.tensor_copy(out=bd_pad[0:2, :], in_=bd_stage[:])
+        rf = const.tile([P, 2, 2], F32, name="rf")
+        nc.vector.tensor_copy(out=rf[:], in_=r_stage[:])
+        pr = ps1p.tile([P, 2, P], BF16, name="pr", tag="ps1")
+        for i in range(2):
+            nc.tensor.transpose(out=pr[:, i, :], in_=r_pad_v[:, i, :], identity=ident[:])
+        pb = ps1p.tile([P, 2, P], BF16, name="pb", tag="ps1")
+        for s in range(2):
+            nc.tensor.transpose(
+                out=pb[:, s, :], in_=bias_d_v[:, s, :], identity=ident[:]
+            )
+
+        regroup(0)
+
+        r_t = const.tile([P, 2, P], BF16, name="r_t")
+        nc.vector.tensor_copy(out=r_t[:], in_=pr[:])
+        bg = const.tile([P, 32], F32, name="bg")
+        nc.vector.tensor_copy(out=bg[:], in_=pb[:, 0, 0:32])
+        b7 = const.tile([P, 32], F32, name="b7")
+        nc.vector.tensor_scalar(
+            out=b7[:], in0=pb[:, 1, 0:32], scalar1=LIMIT, scalar2=None, op0=ALU.add
+        )
+
+        b_sb = const.tile([P, 2, 1024], F32, name="b_sb")
+        new_acc()
+        for k in range(4):
+            hh, i = divmod(k, 2)
+            nc.tensor.matmul(
+                out=acc_of[k][:],
+                lhsT=r_t[:, i, :],
+                rhs=bd_pad[:, 512 * hh : 512 * hh + 512],
+                start=True,
+                stop=True,
+            )
+            nc.scalar.copy(out=b_sb[:, i, 512 * hh : 512 * hh + 512], in_=acc_of[k][:])
+
+        quantise(0, 1)
+
+        xg = const.tile([P, 2, 256, 4], BF16, name="xg", align_bytes=64)
+        xw = const.tile([P, 512], U32, name="xw", align_bytes=64)
+        xs = const.tile([P, 512], U8, name="xs", align_bytes=64)
+        for c in range(2):
+            xt = ps1p.tile([P, 4, 256], BF16, name="xt", tag="ps1")
+            for t in range(4):
+                for i in range(2):
+                    k0 = 512 * c + P * t
+                    nc.tensor.transpose(
+                        out=xt[:, t, P * i : P * i + P],
+                        in_=x_sb[:, i, k0 : k0 + P],
+                        identity=ident[:],
+                    )
+            nc.vector.tensor_copy(
+                out=xg[:, c, :, :], in_=xt.rearrange("p t k -> p k t")
+            )
+
+        regroup(1)
+        nc.vector.quantize_mx(
+            out=xw[:].bitcast(FP8X4),
+            scales=xs[:],
+            in_=xg.rearrange("p c k t -> p (c k t)"),
+        )
+
+        pend_acts = {}
+        pend_epi = {}
+        pend_hq = {}
+        pend_fin = {}
+
+        def quantise_and_multiply(uq, slot):
+            kind, e, g, c = units[uq]
+            quantise(uq, 2 if uq == n_units - 1 else 1)
+            if kind == "A" and c == 1:
+                stage1(e, g, uq)
+                pend_acts[uq + LAG_ACT] = (e, g)
+                pend_epi[uq + LAG_EPI] = (e, g)
+            if kind == "D":
+                stage2(e, g, uq)
+                if g == 3:
+                    if e == 0:
+                        pend_fin[slot + 1] = e
+                    else:
+                        finals(e)
+
+        for slot in range(2, n_units + 8):
+            u = slot
+            if slot <= HEAD_SLOTS:
+                quantise_and_multiply(slot - 1, slot)
+            if u < n_units:
+                if u % 2 == 0:
+                    k = u // 2 + RAW_BUFS - 1
+                    if k < n_chunks:
+                        load_chunk(k)
+                regroup(u)
+            if slot in pend_acts:
+                acts(*pend_acts[slot])
+            if slot in pend_hq:
+                hid_quantise(*pend_hq[slot])
+            if slot in pend_epi:
+                epilogue(*pend_epi[slot])
+                pend_hq[slot + 1] = pend_epi[slot]
+            if slot in pend_fin:
+                finals(pend_fin[slot])
+            if slot > HEAD_SLOTS and slot - 1 < n_units:
+                quantise_and_multiply(slot - 1, slot)

@@ -22,8 +22,8 @@ GLU_CAP = LIMIT / (1.0 + math.exp(-ALPHA * LIMIT))
 
 PIN = True
 RAW_BUFS = 5
-NV_A = 512
-NV_D = 512
+NV_A = 448
+NV_D = 448
 LAG_ACT = 2
 LAG_EPI = 4
 HEAD_SLOTS = 4

@@ -20,7 +20,7 @@ ALPHA = 1.702
 LIMIT = 7.0
 GLU_CAP = LIMIT / (1.0 + math.exp(-ALPHA * LIMIT))
 
-PIN = True
+PIN = False
 RAW_BUFS = 5
 NV_A = 448
 NV_D = 448

@@ -22,8 +22,8 @@ GLU_CAP = LIMIT / (1.0 + math.exp(-ALPHA * LIMIT))
 
 PIN = False
 RAW_BUFS = 5
-NV_A = 448
-NV_D = 448
+NV_A = 512
+NV_D = (448, 352)
 LAG_ACT = 2
 LAG_EPI = 4
 HEAD_SLOTS = 4
@@ -139,9 +139,17 @@ def tile_referenceexperts_kernel(
             else:
                 sv = src.rearrange("p t (q i) -> p q t i", i=4)
                 dv = grp.rearrange("p (q i t) -> p q t i", i=4, t=4)
-                qv = NV_D // 4
-                nc.scalar.copy(out=dv[:, qv:], in_=sv[:, qv:])
-                nc.vector.tensor_copy(out=dv[:, :qv], in_=sv[:, :qv])
+                parts = 2 if u == n_units - 1 else 1
+                span = 256 // parts
+                qv = NV_D[units[u][1]] // (4 * parts)
+                for h in range(parts):
+                    q0 = span * h
+                    nc.scalar.copy(
+                        out=dv[:, q0 + qv : q0 + span], in_=sv[:, q0 + qv : q0 + span]
+                    )
+                    nc.vector.tensor_copy(
+                        out=dv[:, q0 : q0 + qv], in_=sv[:, q0 : q0 + qv]
+                    )
 
         def quantise(u, parts):
             grp = grp_of[u]

@@ -134,8 +134,9 @@ def tile_referenceexperts_kernel(
                 qv = NV_A // 8
                 for s in range(2):
                     nc.scalar.copy(out=dv[:, s, qv:], in_=sv[:, s, qv:])
-                for s in range(2):
-                    nc.vector.tensor_copy(out=dv[:, s, :qv], in_=sv[:, s, :qv])
+                sv4 = src.rearrange("p t (q i s) -> p q t i s", i=2, s=2)
+                dv4 = grp.rearrange("p (s q i t) -> p q t i s", s=2, i=2, t=4)
+                nc.vector.tensor_copy(out=dv4[:, : 2 * qv], in_=sv4[:, : 2 * qv])
             else:
                 sv = src.rearrange("p t (q i) -> p q t i", i=4)
                 dv = grp.rearrange("p (q i t) -> p q t i", i=4, t=4)

@@ -131,12 +131,15 @@ def tile_referenceexperts_kernel(
             if kind == "A":
                 sv = src.rearrange("p t (q i s) -> p s q t i", i=4, s=2)
                 dv = grp.rearrange("p (s q i t) -> p s q t i", s=2, i=4, t=4)
-                qv = NV_A // 8
-                for s in range(2):
-                    nc.scalar.copy(out=dv[:, s, qv:], in_=sv[:, s, qv:])
-                sv4 = src.rearrange("p t (q i s) -> p q t i s", i=2, s=2)
-                dv4 = grp.rearrange("p (s q i t) -> p q t i s", s=2, i=2, t=4)
-                nc.vector.tensor_copy(out=dv4[:, : 2 * qv], in_=sv4[:, : 2 * qv])
+                if u == 0:
+                    qv = NV_A // 8
+                    for s in range(2):
+                        nc.scalar.copy(out=dv[:, s, qv:], in_=sv[:, s, qv:])
+                    for s in range(2):
+                        nc.vector.tensor_copy(out=dv[:, s, :qv], in_=sv[:, s, :qv])
+                else:
+                    nc.scalar.copy(out=dv[:, 1], in_=sv[:, 1])
+                    nc.vector.tensor_copy(out=dv[:, 0], in_=sv[:, 0])
             else:
                 sv = src.rearrange("p t (q i) -> p q t i", i=4)
                 dv = grp.rearrange("p (q i t) -> p q t i", i=4, t=4)

import math
from contextlib import ExitStack

import concourse.mybir as mybir
from concourse.masks import make_identity

FLOPS = 2 * 2 * 256 * 1024 * 4096 + 2 * 2 * 256 * 2048 * 1024

BF16 = mybir.dt.bfloat16
F32 = mybir.dt.float32
I32 = mybir.dt.int32
U32 = mybir.dt.uint32
U8 = mybir.dt.uint8
FP8X4 = mybir.dt.float8_e4m3fn_x4
ACT = mybir.ActivationFunctionType
ALU = mybir.AluOpType

P = 128
ALPHA = 1.702
LIMIT = 7.0
GLU_CAP = LIMIT / (1.0 + math.exp(-ALPHA * LIMIT))

PIN = False
RAW_BUFS = 5
NV_A = 512
NV_D = (448, 352)
LAG_ACT = 2
LAG_EPI = 4
HEAD_SLOTS = 4


def tile_referenceexperts_kernel(
    tc,
    hidden_states,
    routing_weights,
    gate_up_proj,
    gate_up_proj_bias,
    down_proj,
    down_proj_bias,
    out,
):
    nc = tc.nc
    with ExitStack() as ctx:
        const = ctx.enter_context(tc.tile_pool(name="const", bufs=1))
        rawp = ctx.enter_context(tc.tile_pool(name="rawp", bufs=RAW_BUFS))
        grpp = ctx.enter_context(tc.tile_pool(name="grpp", bufs=4))
        codep = ctx.enter_context(tc.tile_pool(name="codep", bufs=8))
        epip = ctx.enter_context(tc.tile_pool(name="epip", bufs=2))
        hidp = ctx.enter_context(tc.tile_pool(name="hidp", bufs=8))
        ps1p = ctx.enter_context(tc.psum_pool(name="ps1p", bufs=4))
        accp = ctx.enter_context(tc.psum_pool(name="accp", bufs=1))
        if PIN:
            ctx.enter_context(tc.manual_schedule())

        wgu = gate_up_proj.rearrange("e (r p) n -> e p r n", p=P)
        wd = down_proj.rearrange("e (r p) h -> e p r h", p=P)
        out_v = out.rearrange("b s h -> s b h")

        units = []
        for e in range(2):
            for g in range(4):
                for c in range(2):
                    units.append(("A", e, g, c))
            for g in range(4):
                units.append(("D", e, g, 0))
        n_units = len(units)
        n_chunks = n_units // 2

        raw_of = {}
        grp_of = {}
        codes_of = {}
        ps_of = {}
        gr_of = {}
        hg_of = {}
        hid_of = {}
        acc_of = {}

        r_stage = const.tile([P, 2, 2], BF16, name="r_stage")
        bias_stage = const.tile([32, 256], BF16, name="bias_stage")
        bd_stage = const.tile([2, 1024], BF16, name="bd_stage")
        nc.scalar.dma_start(
            out=r_stage[:], in_=routing_weights.rearrange("(i p) e -> p i e", p=P)
        )
        nc.scalar.dma_start(
            out=bias_stage[:],
            in_=gate_up_proj_bias.rearrange("e (r q) -> (e r) q", q=256),
        )
        nc.scalar.dma_start(out=bd_stage[:], in_=down_proj_bias)

        zero1 = const.tile([P, 1], F32, name="zero1")
        nc.vector.memset(zero1[:], 0.0)
        warm = const.tile([P, 1], F32, name="warm")
        nc.scalar.activation(out=warm[:], in_=zero1[:], func=ACT.Gelu_apprx_sigmoid)

        bias_d = const.tile([P, 256], BF16, name="bias_d")
        r_pad = const.tile([P, 256], BF16, name="r_pad")
        bd_pad = const.tile([P, 1024], BF16, name="bd_pad")
        nc.vector.memset(r_pad[:].bitcast(I32), 0)
        nc.vector.memset(bias_d[:].bitcast(I32), 0)
        nc.vector.memset(bd_pad[:].bitcast(I32), 0)
        r_pad_v = r_pad.rearrange("p (i k) -> p i k", i=2)
        bias_d_v = bias_d.rearrange("p (s m) -> p s m", s=2)

        ident = const.tile([P, P], BF16, name="ident")
        make_identity(nc, ident[:])

        def chunk_src(k):
            e, kk = divmod(k, n_chunks // 2)
            if kk < 4:
                return wgu[e, :, :, 1024 * kk : 1024 * kk + 1024]
            return wd[e, :, 8 * (kk - 4) : 8 * (kk - 4) + 8, :]

        def new_chunk(k):
            raw_of[k] = rawp.tile([P, 8, 1024], BF16, name="raw")

        def load_piece(k, r0, r1, c0, c1):
            nc.sync.dma_start(
                out=raw_of[k][:, r0:r1, c0:c1], in_=chunk_src(k)[:, r0:r1, c0:c1]
            )

        def load_chunk(k):
            new_chunk(k)
            load_piece(k, 0, 8, 0, 1024)

        def regroup(u):
            kind = units[u][0]
            half = u % 2
            src = raw_of[u // 2][:, 4 * half : 4 * half + 4, :]
            grp = grpp.tile([P, 4096], BF16, name="grp", align_bytes=64)
            grp_of[u] = grp
            if kind == "A":
                sv = src.rearrange("p t (q i s) -> p s q t i", i=4, s=2)
                dv = grp.rearrange("p (s q i t) -> p s q t i", s=2, i=4, t=4)
                if u == 0:
                    qv = NV_A // 8
                    for s in range(2):
                        nc.scalar.copy(out=dv[:, s, qv:], in_=sv[:, s, qv:])
                    for s in range(2):
                        nc.vector.tensor_copy(out=dv[:, s, :qv], in_=sv[:, s, :qv])
                else:
                    nc.scalar.copy(out=dv[:, 1], in_=sv[:, 1])
                    nc.vector.tensor_copy(out=dv[:, 0], in_=sv[:, 0])
            else:
                sv = src.rearrange("p t (q i) -> p q t i", i=4)
                dv = grp.rearrange("p (q i t) -> p q t i", i=4, t=4)
                parts = 2 if u == n_units - 1 else 1
                span = 256 // parts
                qv = NV_D[units[u][1]] // (4 * parts)
                for h in range(parts):
                    q0 = span * h
                    nc.scalar.copy(
                        out=dv[:, q0 + qv : q0 + span], in_=sv[:, q0 + qv : q0 + span]
                    )
                    nc.vector.tensor_copy(
                        out=dv[:, q0 : q0 + qv], in_=sv[:, q0 : q0 + qv]
                    )

        def quantise(u, parts):
            grp = grp_of[u]
            cw = codep.tile([P, 1024], U32, name="cw", align_bytes=64)
            cs = codep.tile([P, 1024], U8, name="cs", align_bytes=64)
            codes_of[u] = (cw, cs)
            w = 1024 // parts
            for h in range(parts):
                nc.vector.quantize_mx(
                    out=cw[:, w * h : w * h + w].bitcast(FP8X4),
                    scales=cs[:, w * h : w * h + w],
                    in_=grp[:, 4 * w * h : 4 * w * h + 4 * w],
                )

        def stage1(e, g, u):
            tiles = []
            for j in range(4):
                ps = ps1p.tile([P, 2, 256], F32, name="ps1", tag="ps1")
                tiles.append(ps)
                for s in range(2):
                    off = 512 * s + P * j
                    for c in range(2):
                        cw, cs = codes_of[u - 1 + c]
                        nc.tensor.matmul_mx(
                            out=ps[:, s, :],
                            lhsT=cw[:, off : off + P].bitcast(FP8X4),
                            lhsT_scale=cs[:, off : off + P],
                            rhs=xw[:, 256 * c : 256 * c + 256].bitcast(FP8X4),
                            rhs_scale=xs[:, 256 * c : 256 * c + 256],
                            start=(c == 0),
                            stop=(c == 1),
                        )
            ps_of[(e, g)] = tiles

        def acts(e, g):
            gt = epip.tile([P, 4, 256], F32, name="gt")
            rt = epip.tile([P, 4, 256], F32, name="rt")
            gr_of[(e, g)] = (gt, rt)
            for j in range(4):
                ps = ps_of[(e, g)][j]
                col = 16 * e + 4 * g + j
                nc.scalar.activation(
                    out=gt[:, j, :],
                    in_=ps[:, 0, :],
                    func=ACT.Gelu_apprx_sigmoid,
                    bias=bg[:, col : col + 1],
                )
                nc.scalar.activation(
                    out=rt[:, j, :],
                    in_=ps[:, 1, :],
                    func=ACT.Relu,
                    bias=b7[:, col : col + 1],
                )

        def epilogue(e, g):
            gt, rt = gr_of[(e, g)]
            nc.vector.tensor_scalar(
                out=rt[:],
                in0=rt[:],
                scalar1=2.0 * LIMIT,
                scalar2=1.0 - LIMIT,
                op0=ALU.min,
                op1=ALU.add,
            )
            hf = epip.tile([P, 4, 256], BF16, name="hf")
            nc.vector.scalar_tensor_tensor(
                out=hf[:],
                in0=gt[:],
                scalar=GLU_CAP,
                in1=rt[:],
                op0=ALU.min,
                op1=ALU.mult,
            )
            hg = epip.tile([P, 1024], BF16, name="hg", align_bytes=64)
            hg_of[(e, g)] = hg
            nc.vector.tensor_copy(
                out=hg.rearrange("p (q i j) -> p q j i", i=4, j=4),
                in_=hf.rearrange("p j (q i) -> p q j i", i=4),
            )

        def hid_quantise(e, g):
            hw = hidp.tile([P, 256], U32, name="hw", align_bytes=64)
            hs = hidp.tile([P, 256], U8, name="hs", align_bytes=64)
            hid_of[(e, g)] = (hw, hs)
            nc.vector.quantize_mx(
                out=hw[:].bitcast(FP8X4), scales=hs[:], in_=hg_of[(e, g)][:]
            )

        def new_acc():
            for k in range(4):
                acc_of[k] = accp.tile([P, 512], F32, name="acc%d" % k)

        def stage2(e, g, u):
            if g == 0:
                new_acc()
            hw, hs = hid_of[(e, g)]
            cw, cs = codes_of[u]
            for k in range(4):
                hh, i = divmod(k, 2)
                nc.tensor.matmul_mx(
                    out=acc_of[k][:],
                    lhsT=hw[:, P * i : P * i + P].bitcast(FP8X4),
                    lhsT_scale=hs[:, P * i : P * i + P],
                    rhs=cw[:, 512 * hh : 512 * hh + 512].bitcast(FP8X4),
                    rhs_scale=cs[:, 512 * hh : 512 * hh + 512],
                    start=(g == 0),
                    stop=(g == 3),
                )

        def finals(e):
            for k in range(4):
                hh, i = divmod(k, 2)
                sl = slice(512 * hh, 512 * hh + 512)
                nc.vector.scalar_tensor_tensor(
                    out=b_sb[:, i, sl],
                    in0=acc_of[k][:],
                    scalar=rf[:, i, e : e + 1],
                    in1=b_sb[:, i, sl],
                    op0=ALU.mult,
                    op1=ALU.add,
                )
                if e == 1:
                    nc.sync.dma_start(out=out_v[:, i, sl], in_=b_sb[:, i, sl])

        x_sb = const.tile([P, 2, 1024], BF16, name="x_sb")
        new_chunk(0)
        load_piece(0, 0, 4, NV_A, 1024)
        load_piece(0, 0, 4, 0, NV_A)
        nc.sync.dma_start(out=x_sb[:], in_=hidden_states.rearrange("b s h -> s b h"))
        load_piece(0, 4, 8, 0, 1024)
        new_chunk(1)
        load_piece(1, 0, 4, 0, 1024)
        load_piece(1, 4, 8, 0, 1024)
        for k in range(2, RAW_BUFS):
            load_chunk(k)

        nc.vector.tensor_copy(out=r_pad_v[:, :, 0:2], in_=r_stage[:])
        nc.vector.tensor_copy(
            out=bias_d_v[0:32, :, :],
            in_=bias_stage.rearrange("p (m s) -> p s m", s=2),
        )
        nc.vector.tensor_copy(out=bd_pad[0:2, :], in_=bd_stage[:])
        rf = const.tile([P, 2, 2], F32, name="rf")
        nc.vector.tensor_copy(out=rf[:], in_=r_stage[:])
        pr = ps1p.tile([P, 2, P], BF16, name="pr", tag="ps1")
        for i in range(2):
            nc.tensor.transpose(out=pr[:, i, :], in_=r_pad_v[:, i, :], identity=ident[:])
        pb = ps1p.tile([P, 2, P], BF16, name="pb", tag="ps1")
        for s in range(2):
            nc.tensor.transpose(
                out=pb[:, s, :], in_=bias_d_v[:, s, :], identity=ident[:]
            )

        regroup(0)

        r_t = const.tile([P, 2, P], BF16, name="r_t")
        nc.vector.tensor_copy(out=r_t[:], in_=pr[:])
        bg = const.tile([P, 32], F32, name="bg")
        nc.vector.tensor_copy(out=bg[:], in_=pb[:, 0, 0:32])
        b7 = const.tile([P, 32], F32, name="b7")
        nc.vector.tensor_scalar(
            out=b7[:], in0=pb[:, 1, 0:32], scalar1=LIMIT, scalar2=None, op0=ALU.add
        )

        b_sb = const.tile([P, 2, 1024], F32, name="b_sb")
        new_acc()
        for k in range(4):
            hh, i = divmod(k, 2)
            nc.tensor.matmul(
                out=acc_of[k][:],
                lhsT=r_t[:, i, :],
                rhs=bd_pad[:, 512 * hh : 512 * hh + 512],
                start=True,
                stop=True,
            )
            nc.scalar.copy(out=b_sb[:, i, 512 * hh : 512 * hh + 512], in_=acc_of[k][:])

        quantise(0, 1)

        xg = const.tile([P, 2, 256, 4], BF16, name="xg", align_bytes=64)
        xw = const.tile([P, 512], U32, name="xw", align_bytes=64)
        xs = const.tile([P, 512], U8, name="xs", align_bytes=64)
        for c in range(2):
            xt = ps1p.tile([P, 4, 256], BF16, name="xt", tag="ps1")
            for t in range(4):
                for i in range(2):
                    k0 = 512 * c + P * t
                    nc.tensor.transpose(
                        out=xt[:, t, P * i : P * i + P],
                        in_=x_sb[:, i, k0 : k0 + P],
                        identity=ident[:],
                    )
            nc.vector.tensor_copy(
                out=xg[:, c, :, :], in_=xt.rearrange("p t k -> p k t")
            )

        regroup(1)
        nc.vector.quantize_mx(
            out=xw[:].bitcast(FP8X4),
            scales=xs[:],
            in_=xg.rearrange("p c k t -> p (c k t)"),
        )

        pend_acts = {}
        pend_epi = {}
        pend_hq = {}
        pend_fin = {}

        def quantise_and_multiply(uq, slot):
            kind, e, g, c = units[uq]
            quantise(uq, 2 if uq == n_units - 1 else 1)
            if kind == "A" and c == 1:
                stage1(e, g, uq)
                pend_acts[uq + LAG_ACT] = (e, g)
                pend_epi[uq + LAG_EPI] = (e, g)
            if kind == "D":
                stage2(e, g, uq)
                if g == 3:
                    if e == 0:
                        pend_fin[slot + 1] = e
                    else:
                        finals(e)

        for slot in range(2, n_units + 8):
            u = slot
            if slot <= HEAD_SLOTS:
                quantise_and_multiply(slot - 1, slot)
            if u < n_units:
                if u % 2 == 0:
                    k = u // 2 + RAW_BUFS - 1
                    if k < n_chunks:
                        load_chunk(k)
                regroup(u)
            if slot in pend_acts:
                acts(*pend_acts[slot])
            if slot in pend_hq:
                hid_quantise(*pend_hq[slot])
            if slot in pend_epi:
                epilogue(*pend_epi[slot])
                pend_hq[slot + 1] = pend_epi[slot]
            if slot in pend_fin:
                finals(pend_fin[slot])
            if slot > HEAD_SLOTS and slot - 1 < n_units:
                quantise_and_multiply(slot - 1, slot)
